import numpy as np
import ml_dtypes


def mxq(x, axis, fmt="e4m3"):
    dtype, down = {"e4m3": (ml_dtypes.float8_e4m3fn, 7), "e5m2": (ml_dtypes.float8_e5m2, 14)}[fmt]
    v = np.moveaxis(np.asarray(x, np.float32).astype(ml_dtypes.bfloat16).astype(np.float64), axis, -1)
    blocks = v.reshape(v.shape[:-1] + (-1, 32))
    amax = np.abs(blocks).max(-1, keepdims=True)
    byte = np.maximum(np.where(amax > 0, np.frexp(amax)[1] - 1 + 127, 0) - down, 1)
    scale = np.exp2(byte - 127.0)
    codes = (blocks / scale).astype(np.float32).astype(dtype).astype(np.float64)
    return np.moveaxis((codes * scale).reshape(v.shape), -1, axis)


WIDE = False


def mx_kscale(k):
    if not WIDE:
        return np.ones(k)
    levels = np.array([10, -10, 5, -5, 0])
    if k % 512:
        return np.exp2(np.random.permutation(np.resize(levels, k // 32))).repeat(32)
    a = np.empty((k // 512, 16))
    for p in range(k // 512):
        a[p, :8] = np.random.permutation(np.resize(levels, 8))
        for g in range(8):
            far = levels[np.abs(levels - a[p, g]) >= 10]
            a[p, g + 8] = far[np.random.randint(len(far))]
    return np.exp2(a.ravel()).repeat(32)


BF16 = ml_dtypes.bfloat16


def bf(x):
    return np.asarray(x, np.float32).astype(BF16)


def f64(x):
    return np.asarray(x).astype(np.float64)


B, N, F, H, O = 16, 512, 512, 128, 512
BN_EPS = 1e-3


def setup_inputs():
    s, t = mx_kscale(F), mx_kscale(N)
    return {'x': bf(np.random.standard_normal((B, N, F)) * s / t[:, None]),
            'adj': bf(np.random.uniform(size=(B, N, N)) * (2.0 / N) * t),
            'w': bf(np.random.standard_normal((F, H)) * (0.22 * np.sqrt(N) / np.sqrt(F)) / s[:, None]),
            'bias': bf(np.random.standard_normal(H) * 0.1),
            'gamma': bf(1.0 + 0.1 * np.random.standard_normal(H)),
            'beta': bf(np.random.standard_normal(H) * 0.1),
            'mean': bf(np.random.standard_normal(H) * 0.1),
            'var': bf(0.01 + 0.02 * np.random.uniform(size=H))}


def reference(x, adj, w, bias, gamma, beta, mean, var):
    xw = mxq(f64(x), 2, 'e4m3') @ mxq(f64(w), 0, 'e4m3')
    agg = mxq(f64(adj), 2, 'e4m3') @ mxq(xw, 1, 'e4m3')
    h = np.maximum(agg + f64(bias), 0.0)
    return (h - f64(mean)) * (f64(gamma) / np.sqrt(f64(var) + BN_EPS)) + f64(beta)

@@ -1,0 +1,204 @@
+from contextlib import ExitStack
+
+import concourse.mybir as mybir
+from concourse.masks import make_identity
+
+B, N, F, H = 16, 512, 512, 128
+BN_EPS = 1e-3
+FLOPS = 2 * B * N * F * H + 2 * B * N * N * H
+
+F32 = mybir.dt.float32
+BF16 = mybir.dt.bfloat16
+U32 = mybir.dt.uint32
+U8 = mybir.dt.uint8
+FP8X4 = mybir.dt.float8_e4m3fn_x4
+ALU = mybir.AluOpType
+ACT = mybir.ActivationFunctionType
+
+P = 128
+XW_DT = F32
+IN_BUFS = 8
+LOOK = IN_BUFS - 1
+
+
+def tile_gnn_pa_t_kernel(tc, x, adj, w, bias, gamma, beta, mean, var, out):
+    nc = tc.nc
+    raw, banks, grouped, codes, scales = {}, {}, {}, {}, {}
+    xw_bank, agg_bank, tmp = {}, {}, {}
+    src = {"x": x, "a": adj}
+
+    with ExitStack() as ctx:
+        const = ctx.enter_context(tc.tile_pool(name="const", bufs=1))
+        inp = ctx.enter_context(tc.tile_pool(name="inp", bufs=IN_BUFS))
+        work = ctx.enter_context(tc.tile_pool(name="work", bufs=3))
+        psum = ctx.enter_context(tc.psum_pool(name="psum", bufs=2))
+        ctx.enter_context(tc.manual_schedule())
+
+        def load(s, pieces):
+            for name in ("x", "a"):
+                t_in = inp.tile([P, 4, 512], BF16, tag="in_" + name, name="in_" + name)
+                view = src[name][s].rearrange("(m t) k -> m t k", t=4)
+                step = 4 // pieces
+                for q in range(pieces):
+                    nc.sync.dma_start(out=t_in[:, q * step:(q + 1) * step, :], in_=view[:, q * step:(q + 1) * step, :])
+                raw[(name, s)] = t_in
+
+        def transposes(s):
+            for name in ("x", "a"):
+                words = raw[(name, s)][:].rearrange("m t k -> m (t k)").bitcast(F32)
+                for j in range(2):
+                    bank = psum.tile([P, 2, 256], F32, tag="tp", bufs=4, name="tp")
+                    for tt in range(2):
+                        t = 2 * j + tt
+                        for u in range(2):
+                            nc.tensor.transpose(
+                                bank[:, u, 128 * tt:128 * (tt + 1)],
+                                words[:, 256 * t + u:256 * (t + 1):2],
+                                ident[:],
+                            )
+                    banks[(name, s, j)] = bank
+
+        def copy_out(name, s, j):
+            if j == 0:
+                g_new = work.tile([P, 2048], BF16, tag="g_" + name, align_bytes=64, name="g_" + name)
+                grouped[(name, s)] = g_new
+            g = grouped[(name, s)]
+            nc.scalar.copy(
+                out=g[:].bitcast(F32)[:, 512 * j:512 * (j + 1)].rearrange("p (c u) -> p c u", u=2),
+                in_=banks[(name, s, j)][:].rearrange("p u c -> p c u"),
+            )
+
+        def quantize(name, s, width, bufs):
+            c_new = work.tile([P, width], U32, tag="c_" + name, bufs=bufs, align_bytes=64, name="c_" + name)
+            s_new = work.tile([P, width], U8, tag="s_" + name, bufs=bufs, align_bytes=64, name="s_" + name)
+            nc.vector.quantize_mx(out=c_new[:].bitcast(FP8X4), scales=s_new[:], in_=grouped[(name, s)][:])
+            codes[(name, s)] = c_new
+            scales[(name, s)] = s_new
+
+        def mx_passes(bank, lname, rname, s, rs):
+            for t in range(4):
+                cols = slice(128 * t, 128 * (t + 1))
+                nc.tensor.matmul_mx(
+                    out=bank[:, t, :],
+                    lhsT=codes[(lname, s)][:, cols].bitcast(FP8X4),
+                    lhsT_scale=scales[(lname, s)][:, cols],
+                    rhs=codes[(rname, rs)][:].bitcast(FP8X4),
+                    rhs_scale=scales[(rname, rs)][:],
+                    start=True,
+                    stop=True,
+                )
+
+        def mm1(s):
+            xw_ps = psum.tile([P, 4, 128], XW_DT, tag="xw", bufs=2, name="xw_ps")
+            mx_passes(xw_ps, "x", "w", s, 0)
+            xw_bank[s] = xw_ps
+
+        def copy_xw(s):
+            g_xw = work.tile([P, 512], BF16, tag="g_xw", align_bytes=64, name="g_xw")
+            nc.scalar.copy(
+                out=g_xw[:].rearrange("p (h t) -> p h t", t=4),
+                in_=xw_bank[s][:].rearrange("p t h -> p h t"),
+            )
+            grouped[("xw", s)] = g_xw
+
+        def mm2(s):
+            agg_ps = psum.tile([P, 4, 128], F32, tag="agg", bufs=2, name="agg_ps")
+            mx_passes(agg_ps, "a", "xw", s, s)
+            agg_bank[s] = agg_ps
+
+        def e1(s):
+            t1 = work.tile([P, 512], F32, tag="t1", name="t1")
+            nc.vector.tensor_tensor(out=t1[:], in0=agg_bank[s][:].rearrange("p t h -> p (t h)"), in1=b4[:], op=ALU.add)
+            tmp[(1, s)] = t1
+
+        def e2(s):
+            t2 = work.tile([P, 512], F32, tag="t2", name="t2")
+            nc.vector.scalar_tensor_tensor(out=t2[:], in0=tmp[(1, s)][:], scalar=0.0, in1=g4[:], op0=ALU.max, op1=ALU.mult)
+            tmp[(2, s)] = t2
+
+        def e3(s):
+            o_t = work.tile([P, 512], F32, tag="o_t", bufs=4, name="o_t")
+            nc.vector.tensor_tensor(out=o_t[:], in0=tmp[(2, s)][:], in1=c4[:], op=ALU.add)
+            nc.sync.dma_start(out=out[s].rearrange("(m t) h -> m (t h)", t=4), in_=o_t[:])
+
+        vecs = const.tile([P, 640], BF16, name="vecs")
+        ones = const.tile([P, P], BF16, name="ones")
+        warm = const.tile([P, 2], F32, name="warm")
+        ident = const.tile([P, P], F32, name="ident")
+        w_raw = const.tile([P, 4, H], BF16, name="w_raw")
+        w_g = const.tile([P, 4 * H], BF16, align_bytes=64, name="w_g")
+        ve = const.tile([P, H], F32, name="ve")
+        sd = const.tile([P, H], F32, name="sd")
+        rsd = const.tile([P, H], F32, name="rsd")
+        mg = const.tile([P, H], F32, name="mg")
+        b4 = const.tile([P, 4 * H], F32, name="b4")
+        g4 = const.tile([P, 4 * H], F32, name="g4")
+        c4 = const.tile([P, 4 * H], F32, name="c4")
+
+        nc.vector.memset(vecs[:], 0.0)
+        nc.vector.memset(warm[:], 1.0)
+        nc.vector.memset(ones[:], 1.0)
+        for i, v in enumerate((bias, gamma, beta, mean, var)):
+            nc.scalar.dma_start(out=vecs[0:1, H * i:H * (i + 1)], in_=v.rearrange("(o h) -> o h", o=1))
+        nc.scalar.activation(out=warm[:, 1:2], in_=warm[:, 0:1], func=ACT.Sqrt)
+        make_identity(nc, ident[:])
+
+        load(0, 2)
+        nc.sync.dma_start(out=w_raw[:], in_=w.rearrange("(p j) h -> p j h", j=4))
+        for s in range(1, LOOK):
+            load(s, 1)
+
+        for s in range(B + 3):
+            if s < B:
+                transposes(s)
+            if s == 0:
+                cv = psum.tile([P, 512], F32, tag="agg", bufs=2, name="cv")
+                c1 = psum.tile([P, 512], F32, tag="agg", bufs=2, name="c1")
+                nc.tensor.matmul(out=cv[:, 0:H], lhsT=ones[:], rhs=vecs[:, 512:640], start=True, stop=True)
+                nc.tensor.matmul(out=c1[:], lhsT=ones[:], rhs=vecs[:, 0:512], start=True, stop=True)
+            if s + LOOK < B:
+                load(s + LOOK, 1)
+            if s == 1:
+                nc.vector.tensor_scalar_add(out=ve[:], in0=cv[:, 0:H], scalar1=BN_EPS)
+                for t in range(4):
+                    nc.vector.tensor_copy(out=b4[:, H * t:H * (t + 1)], in_=c1[:, 0:H])
+            if s == 2:
+                nc.vector.tensor_tensor(out=mg[:], in0=c1[:, 3 * H:4 * H], in1=g4[:, 0:H], op=ALU.mult)
+            if s >= 3:
+                e1(s - 3)
+            if 2 <= s < B + 2:
+                quantize("xw", s - 2, 128, 2)
+            if s == 2:
+                for t in range(4):
+                    nc.vector.tensor_tensor(out=c4[:, H * t:H * (t + 1)], in0=c1[:, 2 * H:3 * H], in1=mg[:], op=ALU.subtract)
+            if s >= 3:
+                e2(s - 3)
+            if s < B:
+                copy_out("x", s, 0)
+                copy_out("x", s, 1)
+                if s == 1:
+                    nc.scalar.activation(out=sd[:], in_=ve[:], func=ACT.Sqrt)
+                quantize("x", s, 512, 3)
+            if s == 0:
+                nc.vector.tensor_copy(
+                    out=w_g[:].rearrange("p (h j) -> p h j", j=4), in_=w_raw[:].rearrange("p j h -> p h j")
+                )
+                grouped[("w", 0)] = w_g
+            if s == 1:
+                nc.vector.reciprocal(out=rsd[:], in_=sd[:])
+            if s >= 3:
+                e3(s - 3)
+            if s < B:
+                copy_out("a", s, 0)
+                copy_out("a", s, 1)
+                quantize("a", s, 512, 4)
+            if s == 0:
+                quantize("w", 0, 128, 1)
+            if s == 1:
+                for t in range(4):
+                    nc.vector.tensor_tensor(out=g4[:, H * t:H * (t + 1)], in0=c1[:, H:2 * H], in1=rsd[:], op=ALU.mult)
+            if 1 <= s < B + 1:
+                mm1(s - 1)
+                copy_xw(s - 1)
+            if 2 <= s < B + 2:
+                mm2(s - 2)

@@ -19,6 +19,8 @@ P = 128
 XW_DT = F32
 IN_BUFS = 8
 LOOK = IN_BUFS - 1
+N_TURNED = 3
+COLS_STEP = 4
 
 
 def tile_gnn_pa_t_kernel(tc, x, adj, w, bias, gamma, beta, mean, var, out):
@@ -34,18 +36,20 @@ def tile_gnn_pa_t_kernel(tc, x, adj, w, bias, gamma, beta, mean, var, out):
         psum = ctx.enter_context(tc.psum_pool(name="psum", bufs=2))
         ctx.enter_context(tc.manual_schedule())
 
-        def load(s, pieces):
-            for name in ("x", "a"):
-                t_in = inp.tile([P, 4, 512], BF16, tag="in_" + name, name="in_" + name)
-                view = src[name][s].rearrange("(m t) k -> m t k", t=4)
-                step = 4 // pieces
-                for q in range(pieces):
-                    nc.sync.dma_start(out=t_in[:, q * step:(q + 1) * step, :], in_=view[:, q * step:(q + 1) * step, :])
-                raw[(name, s)] = t_in
+        def turned(g):
+            return g >= B - N_TURNED
 
-        def transposes(s):
+        def load(g, name, pieces):
+            t_in = inp.tile([P, 4, 512], BF16, tag="in_" + name, name="in_" + name)
+            view = src[name][g].rearrange("(m t) k -> m t k", t=4)
+            step = 4 // pieces
+            for q in range(pieces):
+                nc.sync.dma_start(out=t_in[:, q * step:(q + 1) * step, :], in_=view[:, q * step:(q + 1) * step, :])
+            raw[(name, g)] = t_in
+
+        def transposes(g):
             for name in ("x", "a"):
-                words = raw[(name, s)][:].rearrange("m t k -> m (t k)").bitcast(F32)
+                words = raw[(name, g)][:].rearrange("m t k -> m (t k)").bitcast(F32)
                 for j in range(2):
                     bank = psum.tile([P, 2, 256], F32, tag="tp", bufs=4, name="tp")
                     for tt in range(2):
@@ -56,70 +60,103 @@ def tile_gnn_pa_t_kernel(tc, x, adj, w, bias, gamma, beta, mean, var, out):
                                 words[:, 256 * t + u:256 * (t + 1):2],
                                 ident[:],
                             )
-                    banks[(name, s, j)] = bank
+                    banks[(name, g, j)] = bank
 
-        def copy_out(name, s, j):
-            if j == 0:
-                g_new = work.tile([P, 2048], BF16, tag="g_" + name, align_bytes=64, name="g_" + name)
-                grouped[(name, s)] = g_new
-            g = grouped[(name, s)]
-            nc.scalar.copy(
-                out=g[:].bitcast(F32)[:, 512 * j:512 * (j + 1)].rearrange("p (c u) -> p c u", u=2),
-                in_=banks[(name, s, j)][:].rearrange("p u c -> p c u"),
-            )
+        def copy_out(name, g):
+            g_new = work.tile([P, 2048], BF16, tag="g_" + name, align_bytes=64, name="g_" + name)
+            for j in range(2):
+                nc.scalar.copy(
+                    out=g_new[:].bitcast(F32)[:, 512 * j:512 * (j + 1)].rearrange("p (c u) -> p c u", u=2),
+                    in_=banks[(name, g, j)][:].rearrange("p u c -> p c u"),
+                )
+            grouped[(name, g)] = g_new
 
-        def quantize(name, s, width, bufs):
+        def quantize(name, g, width, bufs):
             c_new = work.tile([P, width], U32, tag="c_" + name, bufs=bufs, align_bytes=64, name="c_" + name)
             s_new = work.tile([P, width], U8, tag="s_" + name, bufs=bufs, align_bytes=64, name="s_" + name)
-            nc.vector.quantize_mx(out=c_new[:].bitcast(FP8X4), scales=s_new[:], in_=grouped[(name, s)][:])
-            codes[(name, s)] = c_new
-            scales[(name, s)] = s_new
+            nc.vector.quantize_mx(out=c_new[:].bitcast(FP8X4), scales=s_new[:], in_=grouped[(name, g)][:])
+            codes[(name, g)] = c_new
+            scales[(name, g)] = s_new
 
-        def mx_passes(bank, lname, rname, s, rs):
-            for t in range(4):
-                cols = slice(128 * t, 128 * (t + 1))
-                nc.tensor.matmul_mx(
-                    out=bank[:, t, :],
-                    lhsT=codes[(lname, s)][:, cols].bitcast(FP8X4),
-                    lhsT_scale=scales[(lname, s)][:, cols],
-                    rhs=codes[(rname, rs)][:].bitcast(FP8X4),
-                    rhs_scale=scales[(rname, rs)][:],
-                    start=True,
-                    stop=True,
-                )
+        def mx_pass(dst, lkey, lcols, rkey):
+            nc.tensor.matmul_mx(
+                out=dst,
+                lhsT=codes[lkey][:, lcols].bitcast(FP8X4),
+                lhsT_scale=scales[lkey][:, lcols],
+                rhs=codes[rkey][:].bitcast(FP8X4),
+                rhs_scale=scales[rkey][:],
+                start=True,
+                stop=True,
+            )
 
-        def mm1(s):
+        def mm1(g):
             xw_ps = psum.tile([P, 4, 128], XW_DT, tag="xw", bufs=2, name="xw_ps")
-            mx_passes(xw_ps, "x", "w", s, 0)
-            xw_bank[s] = xw_ps
+            for t in range(4):
+                mx_pass(xw_ps[:, t, :], ("x", g), slice(128 * t, 128 * (t + 1)), ("w", 0))
+            xw_bank[g] = xw_ps
 
-        def copy_xw(s):
+        def copy_xw(g):
             g_xw = work.tile([P, 512], BF16, tag="g_xw", align_bytes=64, name="g_xw")
             nc.scalar.copy(
                 out=g_xw[:].rearrange("p (h t) -> p h t", t=4),
-                in_=xw_bank[s][:].rearrange("p t h -> p h t"),
+                in_=xw_bank[g][:].rearrange("p t h -> p h t"),
             )
-            grouped[("xw", s)] = g_xw
+            grouped[("xw", g)] = g_xw
 
-        def mm2(s):
+        def mm2(g):
             agg_ps = psum.tile([P, 4, 128], F32, tag="agg", bufs=2, name="agg_ps")
-            mx_passes(agg_ps, "a", "xw", s, s)
-            agg_bank[s] = agg_ps
+            if turned(g):
+                mx_pass(agg_ps[:].rearrange("p t h -> p (t h)"), ("xw", g), slice(0, 128), ("a", g))
+            else:
+                for t in range(4):
+                    mx_pass(agg_ps[:, t, :], ("a", g), slice(128 * t, 128 * (t + 1)), ("xw", g))
+            agg_bank[g] = agg_ps
 
-        def e1(s):
+        def store(g, o_t):
+            nc.sync.dma_start(out=out[g].rearrange("(m t) h -> m (t h)", t=4), in_=o_t[:])
+
+        def e1(g):
             t1 = work.tile([P, 512], F32, tag="t1", name="t1")
-            nc.vector.tensor_tensor(out=t1[:], in0=agg_bank[s][:].rearrange("p t h -> p (t h)"), in1=b4[:], op=ALU.add)
-            tmp[(1, s)] = t1
+            nc.vector.tensor_tensor(out=t1[:], in0=agg_bank[g][:].rearrange("p t h -> p (t h)"), in1=b4[:], op=ALU.add)
+            tmp[(1, g)] = t1
 
-        def e2(s):
+        def e2(g):
             t2 = work.tile([P, 512], F32, tag="t2", name="t2")
-            nc.vector.scalar_tensor_tensor(out=t2[:], in0=tmp[(1, s)][:], scalar=0.0, in1=g4[:], op0=ALU.max, op1=ALU.mult)
-            tmp[(2, s)] = t2
+            nc.vector.scalar_tensor_tensor(out=t2[:], in0=tmp[(1, g)][:], scalar=0.0, in1=g4[:], op0=ALU.max, op1=ALU.mult)
+            tmp[(2, g)] = t2
 
-        def e3(s):
-            o_t = work.tile([P, 512], F32, tag="o_t", bufs=4, name="o_t")
-            nc.vector.tensor_tensor(out=o_t[:], in0=tmp[(2, s)][:], in1=c4[:], op=ALU.add)
-            nc.sync.dma_start(out=out[s].rearrange("(m t) h -> m (t h)", t=4), in_=o_t[:])
+        def e3(g):
+            o_t = work.tile([P, 512], F32, tag="o_t", bufs=6, name="o_t")
+            nc.vector.tensor_tensor(out=o_t[:], in0=tmp[(2, g)][:], in1=c4[:], op=ALU.add)
+            store(g, o_t)
+
+        def relu_bias(g):
+            r1 = work.tile([P, 512], F32, tag="r1", name="r1")
+            nc.scalar.activation(
+                out=r1[:], in_=agg_bank[g][:].rearrange("p t h -> p (t h)"), func=ACT.Relu, bias=cols[:, 0:1], scale=1.0
+            )
+            tmp[(1, g)] = r1
+
+        def affine(g):
+            r2 = work.tile([P, 512], F32, tag="r2", name="r2")
+            nc.vector.tensor_scalar(
+                out=r2[:], in0=tmp[(1, g)][:], scalar1=cols[:, 1:2], scalar2=cols[:, 2:3], op0=ALU.mult, op1=ALU.add
+            )
+            tmp[(2, g)] = r2
+
+        def turn_back(g):
+            back = psum.tile([P, 4, 128], F32, tag="tp", bufs=4, name="back")
+            for t in range(4):
+                nc.tensor.transpose(back[:, t, :], tmp[(2, g)][:, 128 * t:128 * (t + 1)], ident[:])
+            banks[("o", g)] = back
+
+        def copy_back(g, engine):
+            o_t = work.tile([P, 512], F32, tag="o_t", bufs=6, name="o_t")
+            if engine == "vector":
+                nc.vector.tensor_copy(out=o_t[:], in_=banks[("o", g)][:].rearrange("p t h -> p (t h)"))
+            else:
+                nc.scalar.copy(out=o_t[:], in_=banks[("o", g)][:].rearrange("p t h -> p (t h)"))
+            store(g, o_t)
 
         vecs = const.tile([P, 640], BF16, name="vecs")
         ones = const.tile([P, P], BF16, name="ones")
@@ -134,30 +171,38 @@ def tile_gnn_pa_t_kernel(tc, x, adj, w, bias, gamma, beta, mean, var, out):
         b4 = const.tile([P, 4 * H], F32, name="b4")
         g4 = const.tile([P, 4 * H], F32, name="g4")
         c4 = const.tile([P, 4 * H], F32, name="c4")
+        cols = const.tile([P, 4], F32, name="cols")
 
-        nc.vector.memset(vecs[:], 0.0)
-        nc.vector.memset(warm[:], 1.0)
-        nc.vector.memset(ones[:], 1.0)
-        for i, v in enumerate((bias, gamma, beta, mean, var)):
-            nc.scalar.dma_start(out=vecs[0:1, H * i:H * (i + 1)], in_=v.rearrange("(o h) -> o h", o=1))
+        nc.gpsimd.memset(warm[:], 1.0)
         nc.scalar.activation(out=warm[:, 1:2], in_=warm[:, 0:1], func=ACT.Sqrt)
+        nc.vector.memset(vecs[:], 0.0)
+        nc.vector.memset(ones[:], 1.0)
         make_identity(nc, ident[:])
 
-        load(0, 2)
+        load(0, "x", 4)
+        load(0, "a", 2)
         nc.sync.dma_start(out=w_raw[:], in_=w.rearrange("(p j) h -> p j h", j=4))
-        for s in range(1, LOOK):
-            load(s, 1)
+        for i, v in enumerate((bias, gamma, beta, mean, var)):
+            nc.sync.dma_start(out=vecs[0:1, H * i:H * (i + 1)], in_=v.rearrange("(o h) -> o h", o=1))
+        for g in range(1, LOOK):
+            load(g, "x", 1)
+            load(g, "a", 1)
 
-        for s in range(B + 3):
-            if s < B:
-                transposes(s)
+        for s in range(B):
+            transposes(s)
             if s == 0:
                 cv = psum.tile([P, 512], F32, tag="agg", bufs=2, name="cv")
                 c1 = psum.tile([P, 512], F32, tag="agg", bufs=2, name="c1")
                 nc.tensor.matmul(out=cv[:, 0:H], lhsT=ones[:], rhs=vecs[:, 512:640], start=True, stop=True)
                 nc.tensor.matmul(out=c1[:], lhsT=ones[:], rhs=vecs[:, 0:512], start=True, stop=True)
+            if s == COLS_STEP:
+                ct = psum.tile([P, 4, 128], F32, tag="tp", bufs=4, name="ct")
+                for i, full in enumerate((b4, g4, c4)):
+                    nc.tensor.transpose(ct[:, i, :], full[:, 0:H], ident[:])
+                nc.vector.tensor_copy(out=cols[:, 0:3], in_=ct[:, 0:3, 0])
             if s + LOOK < B:
-                load(s + LOOK, 1)
+                load(s + LOOK, "x", 1)
+                load(s + LOOK, "a", 1)
             if s == 1:
                 nc.vector.tensor_scalar_add(out=ve[:], in0=cv[:, 0:H], scalar1=BN_EPS)
                 for t in range(4):
@@ -166,19 +211,17 @@ def tile_gnn_pa_t_kernel(tc, x, adj, w, bias, gamma, beta, mean, var, out):
                 nc.vector.tensor_tensor(out=mg[:], in0=c1[:, 3 * H:4 * H], in1=g4[:, 0:H], op=ALU.mult)
             if s >= 3:
                 e1(s - 3)
-            if 2 <= s < B + 2:
+            if s >= 2:
                 quantize("xw", s - 2, 128, 2)
             if s == 2:
                 for t in range(4):
                     nc.vector.tensor_tensor(out=c4[:, H * t:H * (t + 1)], in0=c1[:, 2 * H:3 * H], in1=mg[:], op=ALU.subtract)
             if s >= 3:
                 e2(s - 3)
-            if s < B:
-                copy_out("x", s, 0)
-                copy_out("x", s, 1)
-                if s == 1:
-                    nc.scalar.activation(out=sd[:], in_=ve[:], func=ACT.Sqrt)
-                quantize("x", s, 512, 3)
+            copy_out("x", s)
+            if s == 1:
+                nc.scalar.activation(out=sd[:], in_=ve[:], func=ACT.Sqrt)
+            quantize("x", s, 512, 3)
             if s == 0:
                 nc.vector.tensor_copy(
                     out=w_g[:].rearrange("p (h j) -> p h j", j=4), in_=w_raw[:].rearrange("p j h -> p h j")
@@ -188,17 +231,35 @@ def tile_gnn_pa_t_kernel(tc, x, adj, w, bias, gamma, beta, mean, var, out):
                 nc.vector.reciprocal(out=rsd[:], in_=sd[:])
             if s >= 3:
                 e3(s - 3)
-            if s < B:
-                copy_out("a", s, 0)
-                copy_out("a", s, 1)
-                quantize("a", s, 512, 4)
+            copy_out("a", s)
+            quantize("a", s, 512, 4)
             if s == 0:
                 quantize("w", 0, 128, 1)
             if s == 1:
                 for t in range(4):
                     nc.vector.tensor_tensor(out=g4[:, H * t:H * (t + 1)], in0=c1[:, H:2 * H], in1=rsd[:], op=ALU.mult)
-            if 1 <= s < B + 1:
+            if s >= 1:
                 mm1(s - 1)
                 copy_xw(s - 1)
-            if 2 <= s < B + 2:
+            if s >= 2:
                 mm2(s - 2)
+                if turned(s - 2):
+                    relu_bias(s - 2)
+
+        mm1(B - 1)
+        copy_xw(B - 1)
+        quantize("xw", B - 2, 128, 2)
+        mm2(B - 2)
+        relu_bias(B - 2)
+        affine(B - 3)
+        turn_back(B - 3)
+        quantize("xw", B - 1, 128, 2)
+        mm2(B - 1)
+        relu_bias(B - 1)
+        copy_back(B - 3, "vector")
+        affine(B - 2)
+        turn_back(B - 2)
+        affine(B - 1)
+        turn_back(B - 1)
+        copy_back(B - 2, "vector")
+        copy_back(B - 1, "scalar")

@@ -20,6 +20,7 @@ XW_DT = F32
 IN_BUFS = 8
 LOOK = IN_BUFS - 1
 N_TURNED = 3
+TURN_EVERY = 4
 COLS_STEP = 4
 
 
@@ -37,7 +38,7 @@ def tile_gnn_pa_t_kernel(tc, x, adj, w, bias, gamma, beta, mean, var, out):
         ctx.enter_context(tc.manual_schedule())
 
         def turned(g):
-            return g >= B - N_TURNED
+            return g >= B - N_TURNED or g % TURN_EVERY == TURN_EVERY - 1
 
         def load(g, name, pieces):
             t_in = inp.tile([P, 4, 512], BF16, tag="in_" + name, name="in_" + name)
@@ -188,7 +189,7 @@ def tile_gnn_pa_t_kernel(tc, x, adj, w, bias, gamma, beta, mean, var, out):
             load(g, "x", 1)
             load(g, "a", 1)
 
-        for s in range(B):
+        for s in range(B - 1):
             transposes(s)
             if s == 0:
                 cv = psum.tile([P, 512], F32, tag="agg", bufs=2, name="cv")
@@ -210,13 +211,17 @@ def tile_gnn_pa_t_kernel(tc, x, adj, w, bias, gamma, beta, mean, var, out):
             if s == 2:
                 nc.vector.tensor_tensor(out=mg[:], in0=c1[:, 3 * H:4 * H], in1=g4[:, 0:H], op=ALU.mult)
             if s >= 3:
-                e1(s - 3)
+                if turned(s - 3):
+                    affine(s - 3)
+                    turn_back(s - 3)
+                else:
+                    e1(s - 3)
             if s >= 2:
                 quantize("xw", s - 2, 128, 2)
             if s == 2:
                 for t in range(4):
                     nc.vector.tensor_tensor(out=c4[:, H * t:H * (t + 1)], in0=c1[:, 2 * H:3 * H], in1=mg[:], op=ALU.subtract)
-            if s >= 3:
+            if s >= 3 and not turned(s - 3):
                 e2(s - 3)
             copy_out("x", s)
             if s == 1:
@@ -229,10 +234,12 @@ def tile_gnn_pa_t_kernel(tc, x, adj, w, bias, gamma, beta, mean, var, out):
                 grouped[("w", 0)] = w_g
             if s == 1:
                 nc.vector.reciprocal(out=rsd[:], in_=sd[:])
-            if s >= 3:
+            if s >= 3 and not turned(s - 3):
                 e3(s - 3)
             copy_out("a", s)
             quantize("a", s, 512, 4)
+            if s >= 3 and turned(s - 3):
+                copy_back(s - 3, "vector")
             if s == 0:
                 quantize("w", 0, 128, 1)
             if s == 1:
@@ -246,19 +253,32 @@ def tile_gnn_pa_t_kernel(tc, x, adj, w, bias, gamma, beta, mean, var, out):
                 if turned(s - 2):
                     relu_bias(s - 2)
 
+        transposes(B - 1)
+        quantize("xw", B - 3, 128, 2)
+        copy_out("x", B - 1)
+        quantize("x", B - 1, 512, 3)
+        e1(B - 4)
+        copy_out("a", B - 1)
+        quantize("a", B - 1, 512, 4)
+        mm1(B - 2)
+        copy_xw(B - 2)
+        mm2(B - 3)
         mm1(B - 1)
         copy_xw(B - 1)
+        relu_bias(B - 3)
+        e2(B - 4)
         quantize("xw", B - 2, 128, 2)
         mm2(B - 2)
-        relu_bias(B - 2)
-        affine(B - 3)
-        turn_back(B - 3)
         quantize("xw", B - 1, 128, 2)
         mm2(B - 1)
+        e3(B - 4)
+        relu_bias(B - 2)
         relu_bias(B - 1)
-        copy_back(B - 3, "vector")
+        affine(B - 3)
+        turn_back(B - 3)
         affine(B - 2)
         turn_back(B - 2)
+        copy_back(B - 3, "scalar")
         affine(B - 1)
         turn_back(B - 1)
         copy_back(B - 2, "vector")

from contextlib import ExitStack

import concourse.mybir as mybir
from concourse.masks import make_identity

B, N, F, H = 16, 512, 512, 128
BN_EPS = 1e-3
FLOPS = 2 * B * N * F * H + 2 * B * N * N * H

F32 = mybir.dt.float32
BF16 = mybir.dt.bfloat16
U32 = mybir.dt.uint32
U8 = mybir.dt.uint8
FP8X4 = mybir.dt.float8_e4m3fn_x4
ALU = mybir.AluOpType
ACT = mybir.ActivationFunctionType

P = 128
XW_DT = F32
IN_BUFS = 8
LOOK = IN_BUFS - 1
N_TURNED = 3
TURN_EVERY = 4
COLS_STEP = 4


def tile_gnn_pa_t_kernel(tc, x, adj, w, bias, gamma, beta, mean, var, out):
    nc = tc.nc
    raw, banks, grouped, codes, scales = {}, {}, {}, {}, {}
    xw_bank, agg_bank, tmp = {}, {}, {}
    src = {"x": x, "a": adj}

    with ExitStack() as ctx:
        const = ctx.enter_context(tc.tile_pool(name="const", bufs=1))
        inp = ctx.enter_context(tc.tile_pool(name="inp", bufs=IN_BUFS))
        work = ctx.enter_context(tc.tile_pool(name="work", bufs=3))
        psum = ctx.enter_context(tc.psum_pool(name="psum", bufs=2))
        ctx.enter_context(tc.manual_schedule())

        def turned(g):
            return g >= B - N_TURNED or g % TURN_EVERY == TURN_EVERY - 1

        def load(g, name, pieces):
            t_in = inp.tile([P, 4, 512], BF16, tag="in_" + name, name="in_" + name)
            view = src[name][g].rearrange("(m t) k -> m t k", t=4)
            step = 4 // pieces
            for q in range(pieces):
                nc.sync.dma_start(out=t_in[:, q * step:(q + 1) * step, :], in_=view[:, q * step:(q + 1) * step, :])
            raw[(name, g)] = t_in

        def transposes(g):
            for name in ("x", "a"):
                words = raw[(name, g)][:].rearrange("m t k -> m (t k)").bitcast(F32)
                for j in range(2):
                    bank = psum.tile([P, 2, 256], F32, tag="tp", bufs=4, name="tp")
                    for tt in range(2):
                        t = 2 * j + tt
                        for u in range(2):
                            nc.tensor.transpose(
                                bank[:, u, 128 * tt:128 * (tt + 1)],
                                words[:, 256 * t + u:256 * (t + 1):2],
                                ident[:],
                            )
                    banks[(name, g, j)] = bank

        def copy_out(name, g):
            g_new = work.tile([P, 2048], BF16, tag="g_" + name, align_bytes=64, name="g_" + name)
            for j in range(2):
                nc.scalar.copy(
                    out=g_new[:].bitcast(F32)[:, 512 * j:512 * (j + 1)].rearrange("p (c u) -> p c u", u=2),
                    in_=banks[(name, g, j)][:].rearrange("p u c -> p c u"),
                )
            grouped[(name, g)] = g_new

        def quantize(name, g, width, bufs):
            c_new = work.tile([P, width], U32, tag="c_" + name, bufs=bufs, align_bytes=64, name="c_" + name)
            s_new = work.tile([P, width], U8, tag="s_" + name, bufs=bufs, align_bytes=64, name="s_" + name)
            nc.vector.quantize_mx(out=c_new[:].bitcast(FP8X4), scales=s_new[:], in_=grouped[(name, g)][:])
            codes[(name, g)] = c_new
            scales[(name, g)] = s_new

        def mx_pass(dst, lkey, lcols, rkey):
            nc.tensor.matmul_mx(
                out=dst,
                lhsT=codes[lkey][:, lcols].bitcast(FP8X4),
                lhsT_scale=scales[lkey][:, lcols],
                rhs=codes[rkey][:].bitcast(FP8X4),
                rhs_scale=scales[rkey][:],
                start=True,
                stop=True,
            )

        def mm1(g):
            xw_ps = psum.tile([P, 4, 128], XW_DT, tag="xw", bufs=2, name="xw_ps")
            for t in range(4):
                mx_pass(xw_ps[:, t, :], ("x", g), slice(128 * t, 128 * (t + 1)), ("w", 0))
            xw_bank[g] = xw_ps

        def copy_xw(g):
            g_xw = work.tile([P, 512], BF16, tag="g_xw", align_bytes=64, name="g_xw")
            nc.scalar.copy(
                out=g_xw[:].rearrange("p (h t) -> p h t", t=4),
                in_=xw_bank[g][:].rearrange("p t h -> p h t"),
            )
            grouped[("xw", g)] = g_xw

        def mm2(g):
            agg_ps = psum.tile([P, 4, 128], F32, tag="agg", bufs=2, name="agg_ps")
            if turned(g):
                mx_pass(agg_ps[:].rearrange("p t h -> p (t h)"), ("xw", g), slice(0, 128), ("a", g))
            else:
                for t in range(4):
                    mx_pass(agg_ps[:, t, :], ("a", g), slice(128 * t, 128 * (t + 1)), ("xw", g))
            agg_bank[g] = agg_ps

        def store(g, o_t):
            nc.sync.dma_start(out=out[g].rearrange("(m t) h -> m (t h)", t=4), in_=o_t[:])

        def e1(g):
            t1 = work.tile([P, 512], F32, tag="t1", name="t1")
            nc.vector.tensor_tensor(out=t1[:], in0=agg_bank[g][:].rearrange("p t h -> p (t h)"), in1=b4[:], op=ALU.add)
            tmp[(1, g)] = t1

        def e2(g):
            t2 = work.tile([P, 512], F32, tag="t2", name="t2")
            nc.vector.scalar_tensor_tensor(out=t2[:], in0=tmp[(1, g)][:], scalar=0.0, in1=g4[:], op0=ALU.max, op1=ALU.mult)
            tmp[(2, g)] = t2

        def e3(g):
            o_t = work.tile([P, 512], F32, tag="o_t", bufs=6, name="o_t")
            nc.vector.tensor_tensor(out=o_t[:], in0=tmp[(2, g)][:], in1=c4[:], op=ALU.add)
            store(g, o_t)

        def relu_bias(g):
            r1 = work.tile([P, 512], F32, tag="r1", name="r1")
            nc.scalar.activation(
                out=r1[:], in_=agg_bank[g][:].rearrange("p t h -> p (t h)"), func=ACT.Relu, bias=cols[:, 0:1], scale=1.0
            )
            tmp[(1, g)] = r1

        def affine(g):
            r2 = work.tile([P, 512], F32, tag="r2", name="r2")
            nc.vector.tensor_scalar(
                out=r2[:], in0=tmp[(1, g)][:], scalar1=cols[:, 1:2], scalar2=cols[:, 2:3], op0=ALU.mult, op1=ALU.add
            )
            tmp[(2, g)] = r2

        def turn_back(g):
            back = psum.tile([P, 4, 128], F32, tag="tp", bufs=4, name="back")
            for t in range(4):
                nc.tensor.transpose(back[:, t, :], tmp[(2, g)][:, 128 * t:128 * (t + 1)], ident[:])
            banks[("o", g)] = back

        def copy_back(g, engine):
            o_t = work.tile([P, 512], F32, tag="o_t", bufs=6, name="o_t")
            if engine == "vector":
                nc.vector.tensor_copy(out=o_t[:], in_=banks[("o", g)][:].rearrange("p t h -> p (t h)"))
            else:
                nc.scalar.copy(out=o_t[:], in_=banks[("o", g)][:].rearrange("p t h -> p (t h)"))
            store(g, o_t)

        vecs = const.tile([P, 640], BF16, name="vecs")
        ones = const.tile([P, P], BF16, name="ones")
        warm = const.tile([P, 2], F32, name="warm")
        ident = const.tile([P, P], F32, name="ident")
        w_raw = const.tile([P, 4, H], BF16, name="w_raw")
        w_g = const.tile([P, 4 * H], BF16, align_bytes=64, name="w_g")
        ve = const.tile([P, H], F32, name="ve")
        sd = const.tile([P, H], F32, name="sd")
        rsd = const.tile([P, H], F32, name="rsd")
        mg = const.tile([P, H], F32, name="mg")
        b4 = const.tile([P, 4 * H], F32, name="b4")
        g4 = const.tile([P, 4 * H], F32, name="g4")
        c4 = const.tile([P, 4 * H], F32, name="c4")
        cols = const.tile([P, 4], F32, name="cols")

        nc.gpsimd.memset(warm[:], 1.0)
        nc.scalar.activation(out=warm[:, 1:2], in_=warm[:, 0:1], func=ACT.Sqrt)
        nc.vector.memset(vecs[:], 0.0)
        nc.vector.memset(ones[:], 1.0)
        make_identity(nc, ident[:])

        load(0, "x", 4)
        load(0, "a", 2)
        nc.sync.dma_start(out=w_raw[:], in_=w.rearrange("(p j) h -> p j h", j=4))
        for i, v in enumerate((bias, gamma, beta, mean, var)):
            nc.sync.dma_start(out=vecs[0:1, H * i:H * (i + 1)], in_=v.rearrange("(o h) -> o h", o=1))
        for g in range(1, LOOK):
            load(g, "x", 1)
            load(g, "a", 1)

        for s in range(B - 1):
            transposes(s)
            if s == 0:
                cv = psum.tile([P, 512], F32, tag="agg", bufs=2, name="cv")
                c1 = psum.tile([P, 512], F32, tag="agg", bufs=2, name="c1")
                nc.tensor.matmul(out=cv[:, 0:H], lhsT=ones[:], rhs=vecs[:, 512:640], start=True, stop=True)
                nc.tensor.matmul(out=c1[:], lhsT=ones[:], rhs=vecs[:, 0:512], start=True, stop=True)
            if s == COLS_STEP:
                ct = psum.tile([P, 4, 128], F32, tag="tp", bufs=4, name="ct")
                for i, full in enumerate((b4, g4, c4)):
                    nc.tensor.transpose(ct[:, i, :], full[:, 0:H], ident[:])
                nc.vector.tensor_copy(out=cols[:, 0:3], in_=ct[:, 0:3, 0])
            if s + LOOK < B:
                load(s + LOOK, "x", 1)
                load(s + LOOK, "a", 1)
            if s == 1:
                nc.vector.tensor_scalar_add(out=ve[:], in0=cv[:, 0:H], scalar1=BN_EPS)
                for t in range(4):
                    nc.vector.tensor_copy(out=b4[:, H * t:H * (t + 1)], in_=c1[:, 0:H])
            if s == 2:
                nc.vector.tensor_tensor(out=mg[:], in0=c1[:, 3 * H:4 * H], in1=g4[:, 0:H], op=ALU.mult)
            if s >= 3:
                if turned(s - 3):
                    affine(s - 3)
                    turn_back(s - 3)
                else:
                    e1(s - 3)
            if s >= 2:
                quantize("xw", s - 2, 128, 2)
            if s == 2:
                for t in range(4):
                    nc.vector.tensor_tensor(out=c4[:, H * t:H * (t + 1)], in0=c1[:, 2 * H:3 * H], in1=mg[:], op=ALU.subtract)
            if s >= 3 and not turned(s - 3):
                e2(s - 3)
            copy_out("x", s)
            if s == 1:
                nc.scalar.activation(out=sd[:], in_=ve[:], func=ACT.Sqrt)
            quantize("x", s, 512, 3)
            if s == 0:
                nc.vector.tensor_copy(
                    out=w_g[:].rearrange("p (h j) -> p h j", j=4), in_=w_raw[:].rearrange("p j h -> p h j")
                )
                grouped[("w", 0)] = w_g
            if s == 1:
                nc.vector.reciprocal(out=rsd[:], in_=sd[:])
            if s >= 3 and not turned(s - 3):
                e3(s - 3)
            copy_out("a", s)
            quantize("a", s, 512, 4)
            if s >= 3 and turned(s - 3):
                copy_back(s - 3, "vector")
            if s == 0:
                quantize("w", 0, 128, 1)
            if s == 1:
                for t in range(4):
                    nc.vector.tensor_tensor(out=g4[:, H * t:H * (t + 1)], in0=c1[:, H:2 * H], in1=rsd[:], op=ALU.mult)
            if s >= 1:
                mm1(s - 1)
                copy_xw(s - 1)
            if s >= 2:
                mm2(s - 2)
                if turned(s - 2):
                    relu_bias(s - 2)

        transposes(B - 1)
        quantize("xw", B - 3, 128, 2)
        copy_out("x", B - 1)
        quantize("x", B - 1, 512, 3)
        e1(B - 4)
        copy_out("a", B - 1)
        quantize("a", B - 1, 512, 4)
        mm1(B - 2)
        copy_xw(B - 2)
        mm2(B - 3)
        mm1(B - 1)
        copy_xw(B - 1)
        relu_bias(B - 3)
        e2(B - 4)
        quantize("xw", B - 2, 128, 2)
        mm2(B - 2)
        quantize("xw", B - 1, 128, 2)
        mm2(B - 1)
        e3(B - 4)
        relu_bias(B - 2)
        relu_bias(B - 1)
        affine(B - 3)
        turn_back(B - 3)
        affine(B - 2)
        turn_back(B - 2)
        copy_back(B - 3, "scalar")
        affine(B - 1)
        turn_back(B - 1)
        copy_back(B - 2, "vector")
        copy_back(B - 1, "scalar")
